import numpy as np
import ml_dtypes

BF16 = ml_dtypes.bfloat16


def bf(x):
    return np.asarray(x, np.float32).astype(BF16)


def f32(x):
    return np.asarray(x, np.float32)


def f64(x):
    return np.asarray(x).astype(np.float64)


def striped(idx):
    return np.tile(idx.reshape(-1, 16).T, (8, 1))


C, S, P, T, NB, F1, F2, N, K, RUN = 512, 4096, 2, 4, 1024, 1024, 512, 8192, 4, 2048


def setup_inputs():
    assert N == P * T * NB == K * RUN
    x = f32(0.5 * np.random.standard_normal((C, S)))
    fc1_w = bf(np.random.standard_normal((P * C, F1)) * np.sqrt(2.0 / (P * C)))
    bias1 = f32(0.1 * np.random.standard_normal((F1, 1)))
    fc2_w = bf(np.random.standard_normal((F1, F2)) * np.sqrt(2.0 / F1))
    bias2 = f32(0.1 * np.random.standard_normal((F2, 1)))
    idx = np.concatenate([np.random.permutation(S)[:RUN] for _ in range(K)])
    return {"x": x, "fc1_w": fc1_w, "bias1": bias1, "fc2_w": fc2_w, "bias2": bias2, "offs": striped(idx)}


def reference(x, fc1_w, bias1, fc2_w, bias2, offs):
    idx = offs[:16].T.reshape(-1)
    acc = f64(x)[:, idx].reshape(C, P, T, NB).sum(axis=2)
    a = np.maximum(acc, 0.0)
    h1 = np.maximum(f64(fc1_w)[:C].T @ a[:, 0] + f64(fc1_w)[C:].T @ a[:, 1] + f64(bias1), 0.0)
    return np.maximum(f64(fc2_w).T @ h1 + f64(bias2), 0.0)

@@ -1,0 +1,96 @@
+import concourse.mybir as mybir
+
+F32, BF16, U16 = mybir.dt.float32, mybir.dt.bfloat16, mybir.dt.uint16
+ADD = mybir.AluOpType.add
+RELU = mybir.ActivationFunctionType.Relu
+
+P = 128
+CHANNELS, FEATURES = 512, 4096
+SIDES, BAG, POSITIONS = 2, 4, 1024
+HIDDEN, OUTPUTS = 1024, 512
+ENTRIES = SIDES * BAG * POSITIONS
+
+CHANNEL_BLOCKS = CHANNELS // P
+HIDDEN_BLOCKS = HIDDEN // P
+OUTPUT_BLOCKS = OUTPUTS // P
+WIDTH = 512
+
+FLOPS = 2 * POSITIONS * (SIDES * CHANNELS * HIDDEN + HIDDEN * OUTPUTS)
+
+
+def tile_halfkpnetwork_b_kernel(tc, x, fc1_w, bias1, fc2_w, bias2, offs, out):
+    nc = tc.nc
+    with (
+        tc.tile_pool(name="held", bufs=1) as held,
+        tc.tile_pool(name="sums", bufs=6) as sums,
+        tc.tile_pool(name="acts", bufs=4) as acts,
+        tc.tile_pool(name="hidden", bufs=2) as hidden,
+        tc.tile_pool(name="stage", bufs=4) as stage,
+        tc.psum_pool(name="psum", bufs=8) as psum,
+    ):
+        offsets = held.tile([P, ENTRIES // 16], U16, name="offsets")
+        nc.sync.dma_start(offsets[:], offs)
+        table = [held.tile([P, FEATURES], F32, name=f"table{cb}") for cb in range(CHANNEL_BLOCKS)]
+        w1 = held.tile([P, SIDES * CHANNEL_BLOCKS, HIDDEN], BF16, name="w1")
+        w2 = held.tile([P, HIDDEN_BLOCKS, OUTPUTS], BF16, name="w2")
+        nc.sync.dma_start(table[0][:], x[0:P, :])
+        nc.sync.dma_start(w1[:], fc1_w.rearrange("(k p) m -> p k m", p=P))
+        for cb in range(1, CHANNEL_BLOCKS):
+            nc.sync.dma_start(table[cb][:], x[cb * P : (cb + 1) * P, :])
+        nc.sync.dma_start(w2[:], fc2_w.rearrange("(k p) r -> p k r", p=P))
+
+        b1 = held.tile([P, HIDDEN_BLOCKS], F32, name="b1")
+        b2 = held.tile([P, OUTPUT_BLOCKS], F32, name="b2")
+        with nc.allow_non_contiguous_dma(reason="a bias has one float32 to a partition"):
+            nc.scalar.dma_start(b1[:], bias1.rearrange("(a p) o -> p (a o)", p=P))
+            nc.scalar.dma_start(b2[:], bias2.rearrange("(a p) o -> p (a o)", p=P))
+
+        zeros = held.tile([P, WIDTH], F32, name="zeros")
+        nc.gpsimd.memset(zeros[:], 0.0)
+
+        for first in range(0, POSITIONS, WIDTH):
+            h1_psum = [psum.tile([P, WIDTH], F32, name=f"h1_psum{m}", tag="bank") for m in range(HIDDEN_BLOCKS)]
+            for cb in range(CHANNEL_BLOCKS):
+                bag = [zeros, zeros]
+                for t in range(BAG):
+                    for side in range(SIDES):
+                        column = ((side * BAG + t) * POSITIONS + first) // 16
+                        longer = sums.tile([P, WIDTH], F32, name=f"bag{side}")
+                        nc.vector.tensor_tensor(
+                            longer[:],
+                            table[cb][:].indirect(offsets[:, column : column + WIDTH // 16]),
+                            bag[side][:],
+                            ADD,
+                        )
+                        bag[side] = longer
+                for side in range(SIDES):
+                    a = acts.tile([P, WIDTH], BF16, name="a")
+                    nc.scalar.activation(a[:], bag[side][:], RELU)
+                    k = side * CHANNEL_BLOCKS + cb
+                    for m in range(HIDDEN_BLOCKS):
+                        nc.tensor.matmul(
+                            h1_psum[m][:],
+                            w1[:, k, m * P : (m + 1) * P],
+                            a[:],
+                            start=(cb == 0 and side == 0),
+                            stop=(cb == CHANNEL_BLOCKS - 1 and side == SIDES - 1),
+                        )
+
+            h1 = [hidden.tile([P, WIDTH], BF16, name=f"h1_{m}") for m in range(HIDDEN_BLOCKS)]
+            for m in range(HIDDEN_BLOCKS):
+                nc.scalar.activation(h1[m][:], h1_psum[m][:], RELU, bias=b1[:, m : m + 1])
+
+            out_psum = [psum.tile([P, WIDTH], F32, name=f"out_psum{r}", tag="bank") for r in range(OUTPUT_BLOCKS)]
+            for m in range(HIDDEN_BLOCKS):
+                for r in range(OUTPUT_BLOCKS):
+                    nc.tensor.matmul(
+                        out_psum[r][:],
+                        w2[:, m, r * P : (r + 1) * P],
+                        h1[m][:],
+                        start=(m == 0),
+                        stop=(m == HIDDEN_BLOCKS - 1),
+                    )
+            for r in range(OUTPUT_BLOCKS):
+                y = stage.tile([P, WIDTH], F32, name="y")
+                nc.scalar.activation(y[:], out_psum[r][:], RELU, bias=b2[:, r : r + 1])
+                nc.sync.dma_start(out[r * P : (r + 1) * P, first : first + WIDTH], y[:])

@@ -13,7 +13,9 @@ ENTRIES = SIDES * BAG * POSITIONS
 CHANNEL_BLOCKS = CHANNELS // P
 HIDDEN_BLOCKS = HIDDEN // P
 OUTPUT_BLOCKS = OUTPUTS // P
-WIDTH = 512
+
+WIDTHS = (384, 384, 256)
+assert sum(WIDTHS) == POSITIONS
 
 FLOPS = 2 * POSITIONS * (SIDES * CHANNELS * HIDDEN + HIDDEN * OUTPUTS)
 
@@ -23,7 +25,7 @@ def tile_halfkpnetwork_b_kernel(tc, x, fc1_w, bias1, fc2_w, bias2, offs, out):
     with (
         tc.tile_pool(name="held", bufs=1) as held,
         tc.tile_pool(name="sums", bufs=6) as sums,
-        tc.tile_pool(name="acts", bufs=4) as acts,
+        tc.tile_pool(name="acts", bufs=2) as acts,
         tc.tile_pool(name="hidden", bufs=2) as hidden,
         tc.tile_pool(name="stage", bufs=4) as stage,
         tc.psum_pool(name="psum", bufs=8) as psum,
@@ -31,12 +33,12 @@ def tile_halfkpnetwork_b_kernel(tc, x, fc1_w, bias1, fc2_w, bias2, offs, out):
         offsets = held.tile([P, ENTRIES // 16], U16, name="offsets")
         nc.sync.dma_start(offsets[:], offs)
         table = [held.tile([P, FEATURES], F32, name=f"table{cb}") for cb in range(CHANNEL_BLOCKS)]
-        w1 = held.tile([P, SIDES * CHANNEL_BLOCKS, HIDDEN], BF16, name="w1")
-        w2 = held.tile([P, HIDDEN_BLOCKS, OUTPUTS], BF16, name="w2")
-        nc.sync.dma_start(table[0][:], x[0:P, :])
-        nc.sync.dma_start(w1[:], fc1_w.rearrange("(k p) m -> p k m", p=P))
-        for cb in range(1, CHANNEL_BLOCKS):
+        w1 = held.tile([P, SIDES, CHANNEL_BLOCKS, HIDDEN], BF16, name="w1")
+        w1_rows = fc1_w.rearrange("(s b p) m -> p s b m", s=SIDES, b=CHANNEL_BLOCKS, p=P)
+        for cb in range(CHANNEL_BLOCKS):
             nc.sync.dma_start(table[cb][:], x[cb * P : (cb + 1) * P, :])
+            nc.sync.dma_start(w1[:, :, cb, :], w1_rows[:, :, cb, :])
+        w2 = held.tile([P, HIDDEN_BLOCKS, OUTPUTS], BF16, name="w2")
         nc.sync.dma_start(w2[:], fc2_w.rearrange("(k p) r -> p k r", p=P))
 
         b1 = held.tile([P, HIDDEN_BLOCKS], F32, name="b1")
@@ -45,52 +47,52 @@ def tile_halfkpnetwork_b_kernel(tc, x, fc1_w, bias1, fc2_w, bias2, offs, out):
             nc.scalar.dma_start(b1[:], bias1.rearrange("(a p) o -> p (a o)", p=P))
             nc.scalar.dma_start(b2[:], bias2.rearrange("(a p) o -> p (a o)", p=P))
 
-        zeros = held.tile([P, WIDTH], F32, name="zeros")
+        zeros = held.tile([P, max(WIDTHS)], F32, name="zeros")
         nc.gpsimd.memset(zeros[:], 0.0)
 
-        for first in range(0, POSITIONS, WIDTH):
-            h1_psum = [psum.tile([P, WIDTH], F32, name=f"h1_psum{m}", tag="bank") for m in range(HIDDEN_BLOCKS)]
+        first = 0
+        for width in WIDTHS:
+            h1_psum = [psum.tile([P, width], F32, name=f"h1_psum{m}", tag="bank") for m in range(HIDDEN_BLOCKS)]
             for cb in range(CHANNEL_BLOCKS):
-                bag = [zeros, zeros]
+                bag = [zeros[:, :width], zeros[:, :width]]
                 for t in range(BAG):
                     for side in range(SIDES):
                         column = ((side * BAG + t) * POSITIONS + first) // 16
-                        longer = sums.tile([P, WIDTH], F32, name=f"bag{side}")
+                        longer = sums.tile([P, width], F32, name=f"bag{side}")
                         nc.vector.tensor_tensor(
                             longer[:],
-                            table[cb][:].indirect(offsets[:, column : column + WIDTH // 16]),
-                            bag[side][:],
+                            table[cb][:].indirect(offsets[:, column : column + width // 16]),
+                            bag[side],
                             ADD,
                         )
-                        bag[side] = longer
+                        bag[side] = longer[:]
                 for side in range(SIDES):
-                    a = acts.tile([P, WIDTH], BF16, name="a")
-                    nc.scalar.activation(a[:], bag[side][:], RELU)
-                    k = side * CHANNEL_BLOCKS + cb
+                    a = acts.tile([P, width], BF16, name="a")
+                    nc.scalar.activation(a[:], bag[side], RELU)
                     for m in range(HIDDEN_BLOCKS):
                         nc.tensor.matmul(
                             h1_psum[m][:],
-                            w1[:, k, m * P : (m + 1) * P],
+                            w1[:, side, cb, m * P : (m + 1) * P],
                             a[:],
                             start=(cb == 0 and side == 0),
                             stop=(cb == CHANNEL_BLOCKS - 1 and side == SIDES - 1),
                         )
 
-            h1 = [hidden.tile([P, WIDTH], BF16, name=f"h1_{m}") for m in range(HIDDEN_BLOCKS)]
+            h1 = [hidden.tile([P, width], BF16, name=f"h1_{m}") for m in range(HIDDEN_BLOCKS)]
             for m in range(HIDDEN_BLOCKS):
                 nc.scalar.activation(h1[m][:], h1_psum[m][:], RELU, bias=b1[:, m : m + 1])
 
-            out_psum = [psum.tile([P, WIDTH], F32, name=f"out_psum{r}", tag="bank") for r in range(OUTPUT_BLOCKS)]
-            for m in range(HIDDEN_BLOCKS):
-                for r in range(OUTPUT_BLOCKS):
+            for r in range(OUTPUT_BLOCKS):
+                out_psum = psum.tile([P, width], F32, name="out_psum", tag="bank")
+                for m in range(HIDDEN_BLOCKS):
                     nc.tensor.matmul(
-                        out_psum[r][:],
+                        out_psum[:],
                         w2[:, m, r * P : (r + 1) * P],
                         h1[m][:],
                         start=(m == 0),
                         stop=(m == HIDDEN_BLOCKS - 1),
                     )
-            for r in range(OUTPUT_BLOCKS):
-                y = stage.tile([P, WIDTH], F32, name="y")
-                nc.scalar.activation(y[:], out_psum[r][:], RELU, bias=b2[:, r : r + 1])
-                nc.sync.dma_start(out[r * P : (r + 1) * P, first : first + WIDTH], y[:])
+                y = stage.tile([P, width], F32, name="y")
+                nc.scalar.activation(y[:], out_psum[:], RELU, bias=b2[:, r : r + 1])
+                nc.sync.dma_start(out[r * P : (r + 1) * P, first : first + width], y[:])
+            first += width

@@ -14,7 +14,7 @@ CHANNEL_BLOCKS = CHANNELS // P
 HIDDEN_BLOCKS = HIDDEN // P
 OUTPUT_BLOCKS = OUTPUTS // P
 
-WIDTHS = (384, 384, 256)
+WIDTHS = (512, 256, 128, 128)
 assert sum(WIDTHS) == POSITIONS
 
 FLOPS = 2 * POSITIONS * (SIDES * CHANNELS * HIDDEN + HIDDEN * OUTPUTS)
@@ -24,7 +24,7 @@ def tile_halfkpnetwork_b_kernel(tc, x, fc1_w, bias1, fc2_w, bias2, offs, out):
     nc = tc.nc
     with (
         tc.tile_pool(name="held", bufs=1) as held,
-        tc.tile_pool(name="sums", bufs=6) as sums,
+        tc.tile_pool(name="sums", bufs=12) as sums,
         tc.tile_pool(name="acts", bufs=2) as acts,
         tc.tile_pool(name="hidden", bufs=2) as hidden,
         tc.tile_pool(name="stage", bufs=4) as stage,

@@ -14,8 +14,12 @@ CHANNEL_BLOCKS = CHANNELS // P
 HIDDEN_BLOCKS = HIDDEN // P
 OUTPUT_BLOCKS = OUTPUTS // P
 
-WIDTHS = (512, 256, 128, 128)
-assert sum(WIDTHS) == POSITIONS
+WIDE = 512
+NARROW = (256, 128, 128)
+assert WIDE + sum(NARROW) == POSITIONS
+BANK = 512
+
+SHARED = (1, 1, 0)
 
 FLOPS = 2 * POSITIONS * (SIDES * CHANNELS * HIDDEN + HIDDEN * OUTPUTS)
 
@@ -25,7 +29,7 @@ def tile_halfkpnetwork_b_kernel(tc, x, fc1_w, bias1, fc2_w, bias2, offs, out):
     with (
         tc.tile_pool(name="held", bufs=1) as held,
         tc.tile_pool(name="sums", bufs=12) as sums,
-        tc.tile_pool(name="acts", bufs=2) as acts,
+        tc.tile_pool(name="acts", bufs=1) as acts,
         tc.tile_pool(name="hidden", bufs=2) as hidden,
         tc.tile_pool(name="stage", bufs=4) as stage,
         tc.psum_pool(name="psum", bufs=8) as psum,
@@ -44,44 +48,58 @@ def tile_halfkpnetwork_b_kernel(tc, x, fc1_w, bias1, fc2_w, bias2, offs, out):
         b1 = held.tile([P, HIDDEN_BLOCKS], F32, name="b1")
         b2 = held.tile([P, OUTPUT_BLOCKS], F32, name="b2")
         with nc.allow_non_contiguous_dma(reason="a bias has one float32 to a partition"):
-            nc.scalar.dma_start(b1[:], bias1.rearrange("(a p) o -> p (a o)", p=P))
-            nc.scalar.dma_start(b2[:], bias2.rearrange("(a p) o -> p (a o)", p=P))
+            nc.sync.dma_start(b1[:], bias1.rearrange("(a p) o -> p (a o)", p=P))
+            nc.sync.dma_start(b2[:], bias2.rearrange("(a p) o -> p (a o)", p=P))
 
-        zeros = held.tile([P, max(WIDTHS)], F32, name="zeros")
+        zeros = held.tile([P, WIDE], F32, name="zeros")
         nc.gpsimd.memset(zeros[:], 0.0)
 
-        first = 0
-        for width in WIDTHS:
-            h1_psum = [psum.tile([P, width], F32, name=f"h1_psum{m}", tag="bank") for m in range(HIDDEN_BLOCKS)]
-            for cb in range(CHANNEL_BLOCKS):
-                bag = [zeros[:, :width], zeros[:, :width]]
-                for t in range(BAG):
-                    for side in range(SIDES):
-                        column = ((side * BAG + t) * POSITIONS + first) // 16
-                        longer = sums.tile([P, width], F32, name=f"bag{side}")
-                        nc.vector.tensor_tensor(
-                            longer[:],
-                            table[cb][:].indirect(offsets[:, column : column + width // 16]),
-                            bag[side],
-                            ADD,
-                        )
-                        bag[side] = longer[:]
+        def look_up(cb, first, width):
+            bag = [zeros[:, :width], zeros[:, :width]]
+            for t in range(BAG):
                 for side in range(SIDES):
-                    a = acts.tile([P, width], BF16, name="a")
-                    nc.scalar.activation(a[:], bag[side], RELU)
-                    for m in range(HIDDEN_BLOCKS):
-                        nc.tensor.matmul(
-                            h1_psum[m][:],
-                            w1[:, side, cb, m * P : (m + 1) * P],
-                            a[:],
-                            start=(cb == 0 and side == 0),
-                            stop=(cb == CHANNEL_BLOCKS - 1 and side == SIDES - 1),
-                        )
+                    column = ((side * BAG + t) * POSITIONS + first) // 16
+                    longer = sums.tile([P, width], F32, name=f"bag{side}")
+                    nc.vector.tensor_tensor(
+                        longer[:],
+                        table[cb][:].indirect(offsets[:, column : column + width // 16]),
+                        bag[side],
+                        ADD,
+                    )
+                    bag[side] = longer[:]
+            clipped = []
+            for side in range(SIDES):
+                a = acts.tile([P, width], BF16, name=f"a{side}")
+                nc.scalar.activation(a[:], bag[side], RELU)
+                clipped.append(a)
+            return clipped
 
+        def open_banks(width):
+            return [psum.tile([P, BANK], F32, name=f"h1_psum{b}", tag="bank") for b in range(HIDDEN_BLOCKS * width // BANK)]
+
+        def first_layer(banks, width, cb, a, skip):
+            blocks = BANK // width
+            turns = [(side, m) for side in range(SIDES) for m in range(HIDDEN_BLOCKS)]
+            if cb == CHANNEL_BLOCKS - 1:
+                turns = [(side, m) for m in range(HIDDEN_BLOCKS) for side in range(SIDES)]
+            for side, m in turns:
+                place = m % blocks
+                nc.tensor.matmul(
+                    banks[m // blocks][:, place * width : (place + 1) * width],
+                    w1[:, side, cb, m * P : (m + 1) * P],
+                    a[side][:, skip : skip + width],
+                    start=(cb == 0 and side == 0 and place == 0),
+                    stop=(cb == CHANNEL_BLOCKS - 1 and side == SIDES - 1 and place == blocks - 1),
+                )
+
+        def second_layer(banks, first, width):
+            blocks = BANK // width
             h1 = [hidden.tile([P, width], BF16, name=f"h1_{m}") for m in range(HIDDEN_BLOCKS)]
             for m in range(HIDDEN_BLOCKS):
-                nc.scalar.activation(h1[m][:], h1_psum[m][:], RELU, bias=b1[:, m : m + 1])
-
+                place = m % blocks
+                nc.scalar.activation(
+                    h1[m][:], banks[m // blocks][:, place * width : (place + 1) * width], RELU, bias=b1[:, m : m + 1]
+                )
             for r in range(OUTPUT_BLOCKS):
                 out_psum = psum.tile([P, width], F32, name="out_psum", tag="bank")
                 for m in range(HIDDEN_BLOCKS):
@@ -95,4 +113,21 @@ def tile_halfkpnetwork_b_kernel(tc, x, fc1_w, bias1, fc2_w, bias2, offs, out):
                 y = stage.tile([P, width], F32, name="y")
                 nc.scalar.activation(y[:], out_psum[:], RELU, bias=b2[:, r : r + 1])
                 nc.sync.dma_start(out[r * P : (r + 1) * P, first : first + width], y[:])
-            first += width
+
+        banks = open_banks(WIDE)
+        for cb in range(CHANNEL_BLOCKS):
+            first_layer(banks, WIDE, cb, look_up(cb, 0, WIDE), 0)
+        second_layer(banks, 0, WIDE)
+
+        narrow_banks = [open_banks(width) for width in NARROW]
+        firsts = [WIDE + sum(NARROW[:k]) for k in range(len(NARROW))]
+        done = 0
+        for k in range(len(NARROW)):
+            for cb in range(done, done + SHARED[k]):
+                a = look_up(cb, firsts[k], POSITIONS - firsts[k])
+                for later in range(k, len(NARROW)):
+                    first_layer(narrow_banks[later], NARROW[later], cb, a, firsts[later] - firsts[k])
+            done += SHARED[k]
+            for cb in range(done, CHANNEL_BLOCKS):
+                first_layer(narrow_banks[k], NARROW[k], cb, look_up(cb, firsts[k], NARROW[k]), 0)
+            second_layer(narrow_banks[k], firsts[k], NARROW[k])

@@ -1,7 +1,7 @@
 import concourse.mybir as mybir
 
 F32, BF16, U16 = mybir.dt.float32, mybir.dt.bfloat16, mybir.dt.uint16
-ADD = mybir.AluOpType.add
+ADD, MAX = mybir.AluOpType.add, mybir.AluOpType.max
 RELU = mybir.ActivationFunctionType.Relu
 
 P = 128
@@ -77,10 +77,10 @@ def tile_halfkpnetwork_b_kernel(tc, x, fc1_w, bias1, fc2_w, bias2, offs, out):
         def open_banks(width):
             return [psum.tile([P, BANK], F32, name=f"h1_psum{b}", tag="bank") for b in range(HIDDEN_BLOCKS * width // BANK)]
 
-        def first_layer(banks, width, cb, a, skip):
+        def first_layer(banks, width, cb, a, skip, bags_follow=True):
             blocks = BANK // width
             turns = [(side, m) for side in range(SIDES) for m in range(HIDDEN_BLOCKS)]
-            if cb == CHANNEL_BLOCKS - 1:
+            if cb == CHANNEL_BLOCKS - 1 and bags_follow:
                 turns = [(side, m) for m in range(HIDDEN_BLOCKS) for side in range(SIDES)]
             for side, m in turns:
                 place = m % blocks
@@ -92,13 +92,23 @@ def tile_halfkpnetwork_b_kernel(tc, x, fc1_w, bias1, fc2_w, bias2, offs, out):
                     stop=(cb == CHANNEL_BLOCKS - 1 and side == SIDES - 1 and place == blocks - 1),
                 )
 
+        def relu_out_of_psum(on_vector, result, product, bias):
+            if on_vector:
+                nc.vector.tensor_scalar(result, product, bias, 0.0, ADD, MAX)
+            else:
+                nc.scalar.activation(result, product, RELU, bias=bias)
+
         def second_layer(banks, first, width):
+            vector_helps = first + width == POSITIONS
             blocks = BANK // width
             h1 = [hidden.tile([P, width], BF16, name=f"h1_{m}") for m in range(HIDDEN_BLOCKS)]
             for m in range(HIDDEN_BLOCKS):
                 place = m % blocks
-                nc.scalar.activation(
-                    h1[m][:], banks[m // blocks][:, place * width : (place + 1) * width], RELU, bias=b1[:, m : m + 1]
+                relu_out_of_psum(
+                    vector_helps and (m // blocks) % 2 == 1,
+                    h1[m][:],
+                    banks[m // blocks][:, place * width : (place + 1) * width],
+                    b1[:, m : m + 1],
                 )
             for r in range(OUTPUT_BLOCKS):
                 out_psum = psum.tile([P, width], F32, name="out_psum", tag="bank")
@@ -111,7 +121,7 @@ def tile_halfkpnetwork_b_kernel(tc, x, fc1_w, bias1, fc2_w, bias2, offs, out):
                         stop=(m == HIDDEN_BLOCKS - 1),
                     )
                 y = stage.tile([P, width], F32, name="y")
-                nc.scalar.activation(y[:], out_psum[:], RELU, bias=b2[:, r : r + 1])
+                relu_out_of_psum(vector_helps and r % 2 == 1, y[:], out_psum[:], b2[:, r : r + 1])
                 nc.sync.dma_start(out[r * P : (r + 1) * P, first : first + width], y[:])
 
         banks = open_banks(WIDE)
@@ -129,5 +139,5 @@ def tile_halfkpnetwork_b_kernel(tc, x, fc1_w, bias1, fc2_w, bias2, offs, out):
                     first_layer(narrow_banks[later], NARROW[later], cb, a, firsts[later] - firsts[k])
             done += SHARED[k]
             for cb in range(done, CHANNEL_BLOCKS):
-                first_layer(narrow_banks[k], NARROW[k], cb, look_up(cb, firsts[k], NARROW[k]), 0)
+                first_layer(narrow_banks[k], NARROW[k], cb, look_up(cb, firsts[k], NARROW[k]), 0, bags_follow=k < len(NARROW) - 1)
             second_layer(narrow_banks[k], firsts[k], NARROW[k])

@@ -99,30 +99,42 @@ def tile_halfkpnetwork_b_kernel(tc, x, fc1_w, bias1, fc2_w, bias2, offs, out):
                 nc.scalar.activation(result, product, RELU, bias=bias)
 
         def second_layer(banks, first, width):
-            vector_helps = first + width == POSITIONS
+            last_chunk = first + width == POSITIONS
             blocks = BANK // width
             h1 = [hidden.tile([P, width], BF16, name=f"h1_{m}") for m in range(HIDDEN_BLOCKS)]
             for m in range(HIDDEN_BLOCKS):
                 place = m % blocks
                 relu_out_of_psum(
-                    vector_helps and (m // blocks) % 2 == 1,
+                    last_chunk and (m // blocks) % 2 == 1,
                     h1[m][:],
                     banks[m // blocks][:, place * width : (place + 1) * width],
                     b1[:, m : m + 1],
                 )
-            for r in range(OUTPUT_BLOCKS):
-                out_psum = psum.tile([P, width], F32, name="out_psum", tag="bank")
+            together = 1 if last_chunk else OUTPUT_BLOCKS
+            side_by_side = min(together, blocks)
+            for r0 in range(0, OUTPUT_BLOCKS, together):
+                out_banks = [
+                    psum.tile([P, side_by_side * width], F32, name=f"out_psum{b}", tag="bank")
+                    for b in range(together // side_by_side)
+                ]
+                spots = {}
+                for r in range(r0, r0 + together):
+                    place = (r - r0) % side_by_side
+                    spots[r] = out_banks[(r - r0) // side_by_side][:, place * width : (place + 1) * width]
                 for m in range(HIDDEN_BLOCKS):
-                    nc.tensor.matmul(
-                        out_psum[:],
-                        w2[:, m, r * P : (r + 1) * P],
-                        h1[m][:],
-                        start=(m == 0),
-                        stop=(m == HIDDEN_BLOCKS - 1),
-                    )
-                y = stage.tile([P, width], F32, name="y")
-                relu_out_of_psum(vector_helps and r % 2 == 1, y[:], out_psum[:], b2[:, r : r + 1])
-                nc.sync.dma_start(out[r * P : (r + 1) * P, first : first + width], y[:])
+                    for r in range(r0, r0 + together):
+                        place = (r - r0) % side_by_side
+                        nc.tensor.matmul(
+                            spots[r],
+                            w2[:, m, r * P : (r + 1) * P],
+                            h1[m][:],
+                            start=(m == 0 and place == 0),
+                            stop=(m == HIDDEN_BLOCKS - 1 and place == side_by_side - 1),
+                        )
+                for r in range(r0, r0 + together):
+                    y = stage.tile([P, width], F32, name="y")
+                    relu_out_of_psum(last_chunk and r % 2 == 1, y[:], spots[r], b2[:, r : r + 1])
+                    nc.sync.dma_start(out[r * P : (r + 1) * P, first : first + width], y[:])
 
         banks = open_banks(WIDE)
         for cb in range(CHANNEL_BLOCKS):

@@ -134,7 +134,8 @@ def tile_halfkpnetwork_b_kernel(tc, x, fc1_w, bias1, fc2_w, bias2, offs, out):
                 for r in range(r0, r0 + together):
                     y = stage.tile([P, width], F32, name="y")
                     relu_out_of_psum(last_chunk and r % 2 == 1, y[:], spots[r], b2[:, r : r + 1])
-                    nc.sync.dma_start(out[r * P : (r + 1) * P, first : first + width], y[:])
+                    queue = nc.scalar if last_chunk else nc.sync
+                    queue.dma_start(out[r * P : (r + 1) * P, first : first + width], y[:])
 
         banks = open_banks(WIDE)
         for cb in range(CHANNEL_BLOCKS):

@@ -55,6 +55,7 @@ def tile_halfkpnetwork_b_kernel(tc, x, fc1_w, bias1, fc2_w, bias2, offs, out):
         nc.gpsimd.memset(zeros[:], 0.0)
 
         def look_up(cb, first, width):
+            very_last = cb == CHANNEL_BLOCKS - 1 and first + width == POSITIONS and width == NARROW[-1]
             bag = [zeros[:, :width], zeros[:, :width]]
             for t in range(BAG):
                 for side in range(SIDES):
@@ -70,7 +71,10 @@ def tile_halfkpnetwork_b_kernel(tc, x, fc1_w, bias1, fc2_w, bias2, offs, out):
             clipped = []
             for side in range(SIDES):
                 a = acts.tile([P, width], BF16, name=f"a{side}")
-                nc.scalar.activation(a[:], bag[side], RELU)
+                if very_last and side == SIDES - 1:
+                    nc.vector.tensor_scalar_max(a[:], bag[side], 0.0)
+                else:
+                    nc.scalar.activation(a[:], bag[side], RELU)
                 clipped.append(a)
             return clipped
 
@@ -81,7 +85,7 @@ def tile_halfkpnetwork_b_kernel(tc, x, fc1_w, bias1, fc2_w, bias2, offs, out):
             blocks = BANK // width
             turns = [(side, m) for side in range(SIDES) for m in range(HIDDEN_BLOCKS)]
             if cb == CHANNEL_BLOCKS - 1 and bags_follow:
-                turns = [(side, m) for m in range(HIDDEN_BLOCKS) for side in range(SIDES)]
+                turns = [(side, m) for m0 in range(0, HIDDEN_BLOCKS, blocks) for side in range(SIDES) for m in range(m0, m0 + blocks)]
             for side, m in turns:
                 place = m % blocks
                 nc.tensor.matmul(

import concourse.mybir as mybir

F32, BF16, U16 = mybir.dt.float32, mybir.dt.bfloat16, mybir.dt.uint16
ADD, MAX = mybir.AluOpType.add, mybir.AluOpType.max
RELU = mybir.ActivationFunctionType.Relu

P = 128
CHANNELS, FEATURES = 512, 4096
SIDES, BAG, POSITIONS = 2, 4, 1024
HIDDEN, OUTPUTS = 1024, 512
ENTRIES = SIDES * BAG * POSITIONS

CHANNEL_BLOCKS = CHANNELS // P
HIDDEN_BLOCKS = HIDDEN // P
OUTPUT_BLOCKS = OUTPUTS // P

WIDE = 512
NARROW = (256, 128, 128)
assert WIDE + sum(NARROW) == POSITIONS
BANK = 512

SHARED = (1, 1, 0)

FLOPS = 2 * POSITIONS * (SIDES * CHANNELS * HIDDEN + HIDDEN * OUTPUTS)


def tile_halfkpnetwork_b_kernel(tc, x, fc1_w, bias1, fc2_w, bias2, offs, out):
    nc = tc.nc
    with (
        tc.tile_pool(name="held", bufs=1) as held,
        tc.tile_pool(name="sums", bufs=12) as sums,
        tc.tile_pool(name="acts", bufs=1) as acts,
        tc.tile_pool(name="hidden", bufs=2) as hidden,
        tc.tile_pool(name="stage", bufs=4) as stage,
        tc.psum_pool(name="psum", bufs=8) as psum,
    ):
        offsets = held.tile([P, ENTRIES // 16], U16, name="offsets")
        nc.sync.dma_start(offsets[:], offs)
        table = [held.tile([P, FEATURES], F32, name=f"table{cb}") for cb in range(CHANNEL_BLOCKS)]
        w1 = held.tile([P, SIDES, CHANNEL_BLOCKS, HIDDEN], BF16, name="w1")
        w1_rows = fc1_w.rearrange("(s b p) m -> p s b m", s=SIDES, b=CHANNEL_BLOCKS, p=P)
        for cb in range(CHANNEL_BLOCKS):
            nc.sync.dma_start(table[cb][:], x[cb * P : (cb + 1) * P, :])
            nc.sync.dma_start(w1[:, :, cb, :], w1_rows[:, :, cb, :])
        w2 = held.tile([P, HIDDEN_BLOCKS, OUTPUTS], BF16, name="w2")
        nc.sync.dma_start(w2[:], fc2_w.rearrange("(k p) r -> p k r", p=P))

        b1 = held.tile([P, HIDDEN_BLOCKS], F32, name="b1")
        b2 = held.tile([P, OUTPUT_BLOCKS], F32, name="b2")
        with nc.allow_non_contiguous_dma(reason="a bias has one float32 to a partition"):
            nc.sync.dma_start(b1[:], bias1.rearrange("(a p) o -> p (a o)", p=P))
            nc.sync.dma_start(b2[:], bias2.rearrange("(a p) o -> p (a o)", p=P))

        zeros = held.tile([P, WIDE], F32, name="zeros")
        nc.gpsimd.memset(zeros[:], 0.0)

        def look_up(cb, first, width):
            very_last = cb == CHANNEL_BLOCKS - 1 and first + width == POSITIONS and width == NARROW[-1]
            bag = [zeros[:, :width], zeros[:, :width]]
            for t in range(BAG):
                for side in range(SIDES):
                    column = ((side * BAG + t) * POSITIONS + first) // 16
                    longer = sums.tile([P, width], F32, name=f"bag{side}")
                    nc.vector.tensor_tensor(
                        longer[:],
                        table[cb][:].indirect(offsets[:, column : column + width // 16]),
                        bag[side],
                        ADD,
                    )
                    bag[side] = longer[:]
            clipped = []
            for side in range(SIDES):
                a = acts.tile([P, width], BF16, name=f"a{side}")
                if very_last and side == SIDES - 1:
                    nc.vector.tensor_scalar_max(a[:], bag[side], 0.0)
                else:
                    nc.scalar.activation(a[:], bag[side], RELU)
                clipped.append(a)
            return clipped

        def open_banks(width):
            return [psum.tile([P, BANK], F32, name=f"h1_psum{b}", tag="bank") for b in range(HIDDEN_BLOCKS * width // BANK)]

        def first_layer(banks, width, cb, a, skip, bags_follow=True):
            blocks = BANK // width
            turns = [(side, m) for side in range(SIDES) for m in range(HIDDEN_BLOCKS)]
            if cb == CHANNEL_BLOCKS - 1 and bags_follow:
                turns = [(side, m) for m0 in range(0, HIDDEN_BLOCKS, blocks) for side in range(SIDES) for m in range(m0, m0 + blocks)]
            for side, m in turns:
                place = m % blocks
                nc.tensor.matmul(
                    banks[m // blocks][:, place * width : (place + 1) * width],
                    w1[:, side, cb, m * P : (m + 1) * P],
                    a[side][:, skip : skip + width],
                    start=(cb == 0 and side == 0 and place == 0),
                    stop=(cb == CHANNEL_BLOCKS - 1 and side == SIDES - 1 and place == blocks - 1),
                )

        def relu_out_of_psum(on_vector, result, product, bias):
            if on_vector:
                nc.vector.tensor_scalar(result, product, bias, 0.0, ADD, MAX)
            else:
                nc.scalar.activation(result, product, RELU, bias=bias)

        def second_layer(banks, first, width):
            last_chunk = first + width == POSITIONS
            blocks = BANK // width
            h1 = [hidden.tile([P, width], BF16, name=f"h1_{m}") for m in range(HIDDEN_BLOCKS)]
            for m in range(HIDDEN_BLOCKS):
                place = m % blocks
                relu_out_of_psum(
                    last_chunk and (m // blocks) % 2 == 1,
                    h1[m][:],
                    banks[m // blocks][:, place * width : (place + 1) * width],
                    b1[:, m : m + 1],
                )
            together = 1 if last_chunk else OUTPUT_BLOCKS
            side_by_side = min(together, blocks)
            for r0 in range(0, OUTPUT_BLOCKS, together):
                out_banks = [
                    psum.tile([P, side_by_side * width], F32, name=f"out_psum{b}", tag="bank")
                    for b in range(together // side_by_side)
                ]
                spots = {}
                for r in range(r0, r0 + together):
                    place = (r - r0) % side_by_side
                    spots[r] = out_banks[(r - r0) // side_by_side][:, place * width : (place + 1) * width]
                for m in range(HIDDEN_BLOCKS):
                    for r in range(r0, r0 + together):
                        place = (r - r0) % side_by_side
                        nc.tensor.matmul(
                            spots[r],
                            w2[:, m, r * P : (r + 1) * P],
                            h1[m][:],
                            start=(m == 0 and place == 0),
                            stop=(m == HIDDEN_BLOCKS - 1 and place == side_by_side - 1),
                        )
                for r in range(r0, r0 + together):
                    y = stage.tile([P, width], F32, name="y")
                    relu_out_of_psum(last_chunk and r % 2 == 1, y[:], spots[r], b2[:, r : r + 1])
                    queue = nc.scalar if last_chunk else nc.sync
                    queue.dma_start(out[r * P : (r + 1) * P, first : first + width], y[:])

        banks = open_banks(WIDE)
        for cb in range(CHANNEL_BLOCKS):
            first_layer(banks, WIDE, cb, look_up(cb, 0, WIDE), 0)
        second_layer(banks, 0, WIDE)

        narrow_banks = [open_banks(width) for width in NARROW]
        firsts = [WIDE + sum(NARROW[:k]) for k in range(len(NARROW))]
        done = 0
        for k in range(len(NARROW)):
            for cb in range(done, done + SHARED[k]):
                a = look_up(cb, firsts[k], POSITIONS - firsts[k])
                for later in range(k, len(NARROW)):
                    first_layer(narrow_banks[later], NARROW[later], cb, a, firsts[later] - firsts[k])
            done += SHARED[k]
            for cb in range(done, CHANNEL_BLOCKS):
                first_layer(narrow_banks[k], NARROW[k], cb, look_up(cb, firsts[k], NARROW[k]), 0, bags_follow=k < len(NARROW) - 1)
            second_layer(narrow_banks[k], firsts[k], NARROW[k])
